import numpy as np
import ml_dtypes

BF16 = ml_dtypes.bfloat16


def bf(x):
    return np.asarray(x, np.float32).astype(BF16)


def f32(x):
    return np.asarray(x, np.float32)


def f64(x):
    return np.asarray(x).astype(np.float64)


def striped(idx):
    return np.tile(idx.reshape(-1, 16).T, (8, 1))


C, S, N, B, T, NN, L = 512, 4096, 2048, 2, 1024, 512, 32


def setup_inputs():
    table = f32(np.random.standard_normal((C, S)))
    pos = f32(0.5 * np.random.standard_normal((C, T)))
    node = bf(0.5 * np.random.standard_normal((NN, C)))
    st = np.stack([np.random.permutation(T)[:NN] for _ in range(B)], axis=1)
    ln = np.stack([np.random.permutation(np.tile(np.arange(L), NN // L)) for _ in range(B)], axis=1)
    return {"table": table, "pos": pos, "node": node, "starts": f32(st), "ends": f32(np.minimum(st + ln, T - 1)), "offs": striped(np.random.permutation(np.tile(np.arange(S), 2))[:N])}


def reference(table, pos, node, starts, ends, offs):
    idx = offs[:16].T.reshape(-1)
    t = np.arange(T).astype(np.float64)
    x = f64(table)[:, idx] + np.tile(f64(pos), (1, B))
    mask = (f64(starts).T[:, :, None] <= t) & (t <= f64(ends).T[:, :, None])
    span = np.einsum('nc,bnt->cbt', f64(node), mask.astype(np.float64)).reshape(C, N)
    return x + span

@@ -1,0 +1,101 @@
+import concourse.mybir as mybir
+
+F32 = mybir.dt.float32
+BF16 = mybir.dt.bfloat16
+U16 = mybir.dt.uint16
+ALU = mybir.AluOpType
+ABS = mybir.ActivationFunctionType.Abs
+
+P = 128
+FEATURES = 512
+VOCAB = 4096
+SEQS = 2
+POSITIONS = 1024
+TOKENS = SEQS * POSITIONS
+NODES = 512
+FEATURE_BLOCKS = FEATURES // P
+NODE_BLOCKS = NODES // P
+BANK = 512
+BANKS_PER_BLOCK = TOKENS // BANK
+OFFSET_COLS = POSITIONS // 16
+
+FLOPS = 2 * NODES * FEATURES * TOKENS
+
+
+def tile_nodeawaretokenembedder_kernel(tc, table, pos, node, starts, ends, offs, out):
+    nc = tc.nc
+    with (
+        tc.tile_pool(name="held", bufs=1) as held,
+        tc.tile_pool(name="scratch", bufs=2) as scratch,
+        tc.psum_pool(name="psum", bufs=2) as psum,
+    ):
+        offsets = held.tile([P, TOKENS // 16], U16, name="offsets")
+        nc.sync.dma_start(offsets[:], offs)
+
+        starts_sb = held.tile([P, NODE_BLOCKS * SEQS], F32, name="starts_sb")
+        ends_sb = held.tile([P, NODE_BLOCKS * SEQS], F32, name="ends_sb")
+        nc.sync.dma_start(starts_sb[:], starts.rearrange("(p k) b -> p (k b)", k=NODE_BLOCKS))
+        nc.sync.dma_start(ends_sb[:], ends.rearrange("(p k) b -> p (k b)", k=NODE_BLOCKS))
+
+        node_sb = held.tile([P, NODE_BLOCKS, FEATURES], BF16, name="node_sb")
+        pos_sb = []
+        table_sb = []
+        for cb in range(FEATURE_BLOCKS):
+            rows = slice(cb * P, (cb + 1) * P)
+            pos_sb.append(held.tile([P, POSITIONS], F32, name=f"pos{cb}"))
+            nc.sync.dma_start(pos_sb[cb][:], pos[rows, :])
+            table_sb.append(held.tile([P, VOCAB], F32, name=f"table{cb}"))
+            nc.sync.dma_start(table_sb[cb][:], table[rows, :])
+            if cb == 0:
+                nc.sync.dma_start(node_sb[:], node.rearrange("(p k) c -> p k c", k=NODE_BLOCKS))
+
+        position = held.tile([P, POSITIONS], F32, name="position")
+        nc.gpsimd.iota(
+            position[:], pattern=[[1, POSITIONS]], base=0, channel_multiplier=0,
+            allow_small_or_imprecise_dtypes=True,
+        )
+        neg_sum = held.tile([P, NODE_BLOCKS * SEQS], F32, name="neg_sum")
+        nc.vector.scalar_tensor_tensor(
+            out=neg_sum[:], in0=starts_sb[:], scalar=-1.0, in1=ends_sb[:], op0=ALU.mult, op1=ALU.subtract
+        )
+        length = held.tile([P, NODE_BLOCKS * SEQS], F32, name="length")
+        nc.vector.tensor_tensor(length[:], ends_sb[:], starts_sb[:], ALU.subtract)
+
+        mask = []
+        for k in range(NODE_BLOCKS):
+            mask.append(held.tile([P, TOKENS], BF16, name=f"mask{k}"))
+            for b in range(SEQS):
+                col = k * SEQS + b
+                distance = scratch.tile([P, POSITIONS], F32, name="distance")
+                nc.scalar.activation(distance[:], position[:], ABS, bias=neg_sum[:, col : col + 1], scale=2.0)
+                nc.vector.tensor_scalar(
+                    mask[k][:, b * POSITIONS : (b + 1) * POSITIONS], distance[:],
+                    length[:, col : col + 1], None, ALU.is_le,
+                )
+
+        for cb in range(FEATURE_BLOCKS):
+            rows = slice(cb * P, (cb + 1) * P)
+
+            embed = held.tile([P, TOKENS], F32, name=f"embed{cb}")
+            for b in range(SEQS):
+                nc.vector.tensor_tensor(
+                    embed[:, b * POSITIONS : (b + 1) * POSITIONS],
+                    table_sb[cb][:].indirect(offsets[:, b * OFFSET_COLS : (b + 1) * OFFSET_COLS]),
+                    pos_sb[cb][:],
+                    ALU.add,
+                )
+
+            span = [psum.tile([P, BANK], F32, name=f"span{q}") for q in range(BANKS_PER_BLOCK)]
+            for k in range(NODE_BLOCKS):
+                for q in range(BANKS_PER_BLOCK):
+                    nc.tensor.matmul(
+                        span[q][:], node_sb[:, k, rows], mask[k][:, q * BANK : (q + 1) * BANK],
+                        start=(k == 0), stop=(k == NODE_BLOCKS - 1),
+                    )
+
+            for q in range(BANKS_PER_BLOCK):
+                cols = slice(q * BANK, (q + 1) * BANK)
+                nc.vector.tensor_tensor(embed[:, cols], embed[:, cols], span[q][:], ALU.add)
+            for b in range(SEQS):
+                cols = slice(b * POSITIONS, (b + 1) * POSITIONS)
+                nc.sync.dma_start(out[rows, cols], embed[:, cols])

@@ -26,9 +26,13 @@ def tile_nodeawaretokenembedder_kernel(tc, table, pos, node, starts, ends, offs,
     nc = tc.nc
     with (
         tc.tile_pool(name="held", bufs=1) as held,
-        tc.tile_pool(name="scratch", bufs=2) as scratch,
+        tc.tile_pool(name="scratch", bufs=NODE_BLOCKS * SEQS) as scratch,
         tc.psum_pool(name="psum", bufs=2) as psum,
     ):
+        warm = held.tile([P, 1], F32, name="warm")
+        nc.vector.memset(warm[:], 0.0)
+        nc.scalar.activation(warm[:], warm[:], ABS)
+
         offsets = held.tile([P, TOKENS // 16], U16, name="offsets")
         nc.sync.dma_start(offsets[:], offs)
 
@@ -93,9 +97,14 @@ def tile_nodeawaretokenembedder_kernel(tc, table, pos, node, starts, ends, offs,
                         start=(k == 0), stop=(k == NODE_BLOCKS - 1),
                     )
 
+            span_sb = held.tile([P, TOKENS], F32, name=f"span_sb{cb}")
             for q in range(BANKS_PER_BLOCK):
                 cols = slice(q * BANK, (q + 1) * BANK)
-                nc.vector.tensor_tensor(embed[:, cols], embed[:, cols], span[q][:], ALU.add)
+                if q == BANKS_PER_BLOCK - 1:
+                    nc.vector.tensor_tensor(embed[:, cols], embed[:, cols], span[q][:], ALU.add)
+                else:
+                    nc.scalar.copy(span_sb[:, cols], span[q][:])
+                    nc.gpsimd.tensor_tensor(embed[:, cols], embed[:, cols], span_sb[:, cols], ALU.add)
             for b in range(SEQS):
                 cols = slice(b * POSITIONS, (b + 1) * POSITIONS)
                 nc.sync.dma_start(out[rows, cols], embed[:, cols])

@@ -17,6 +17,7 @@ FEATURE_BLOCKS = FEATURES // P
 NODE_BLOCKS = NODES // P
 BANK = 512
 BANKS_PER_BLOCK = TOKENS // BANK
+PSUM_BANKS = 8
 OFFSET_COLS = POSITIONS // 16
 
 FLOPS = 2 * NODES * FEATURES * TOKENS
@@ -26,8 +27,7 @@ def tile_nodeawaretokenembedder_kernel(tc, table, pos, node, starts, ends, offs,
     nc = tc.nc
     with (
         tc.tile_pool(name="held", bufs=1) as held,
-        tc.tile_pool(name="scratch", bufs=NODE_BLOCKS * SEQS) as scratch,
-        tc.psum_pool(name="psum", bufs=2) as psum,
+        tc.psum_pool(name="psum", bufs=PSUM_BANKS) as psum,
     ):
         warm = held.tile([P, 1], F32, name="warm")
         nc.vector.memset(warm[:], 0.0)
@@ -38,10 +38,10 @@ def tile_nodeawaretokenembedder_kernel(tc, table, pos, node, starts, ends, offs,
 
         starts_sb = held.tile([P, NODE_BLOCKS * SEQS], F32, name="starts_sb")
         ends_sb = held.tile([P, NODE_BLOCKS * SEQS], F32, name="ends_sb")
+        node_sb = held.tile([P, NODE_BLOCKS, FEATURES], BF16, name="node_sb")
         nc.sync.dma_start(starts_sb[:], starts.rearrange("(p k) b -> p (k b)", k=NODE_BLOCKS))
         nc.sync.dma_start(ends_sb[:], ends.rearrange("(p k) b -> p (k b)", k=NODE_BLOCKS))
-
-        node_sb = held.tile([P, NODE_BLOCKS, FEATURES], BF16, name="node_sb")
+        nc.sync.dma_start(node_sb[:], node.rearrange("(p k) c -> p k c", k=NODE_BLOCKS))
         pos_sb = []
         table_sb = []
         for cb in range(FEATURE_BLOCKS):
@@ -50,32 +50,36 @@ def tile_nodeawaretokenembedder_kernel(tc, table, pos, node, starts, ends, offs,
             nc.sync.dma_start(pos_sb[cb][:], pos[rows, :])
             table_sb.append(held.tile([P, VOCAB], F32, name=f"table{cb}"))
             nc.sync.dma_start(table_sb[cb][:], table[rows, :])
-            if cb == 0:
-                nc.sync.dma_start(node_sb[:], node.rearrange("(p k) c -> p k c", k=NODE_BLOCKS))
 
         position = held.tile([P, POSITIONS], F32, name="position")
         nc.gpsimd.iota(
             position[:], pattern=[[1, POSITIONS]], base=0, channel_multiplier=0,
             allow_small_or_imprecise_dtypes=True,
         )
+        mask = [held.tile([P, TOKENS], BF16, name=f"mask{k}") for k in range(NODE_BLOCKS)]
+
         neg_sum = held.tile([P, NODE_BLOCKS * SEQS], F32, name="neg_sum")
         nc.vector.scalar_tensor_tensor(
             out=neg_sum[:], in0=starts_sb[:], scalar=-1.0, in1=ends_sb[:], op0=ALU.mult, op1=ALU.subtract
         )
         length = held.tile([P, NODE_BLOCKS * SEQS], F32, name="length")
         nc.vector.tensor_tensor(length[:], ends_sb[:], starts_sb[:], ALU.subtract)
-
-        mask = []
-        for k in range(NODE_BLOCKS):
-            mask.append(held.tile([P, TOKENS], BF16, name=f"mask{k}"))
-            for b in range(SEQS):
+        for b in range(SEQS):
+            for k in range(1, NODE_BLOCKS):
                 col = k * SEQS + b
-                distance = scratch.tile([P, POSITIONS], F32, name="distance")
+                distance = held.tile([P, POSITIONS], F32, name=f"distance{k}_{b}")
                 nc.scalar.activation(distance[:], position[:], ABS, bias=neg_sum[:, col : col + 1], scale=2.0)
                 nc.vector.tensor_scalar(
                     mask[k][:, b * POSITIONS : (b + 1) * POSITIONS], distance[:],
                     length[:, col : col + 1], None, ALU.is_le,
                 )
+        for b in range(SEQS):
+            after_start = held.tile([P, POSITIONS], BF16, name=f"after_start{b}")
+            nc.vector.tensor_scalar(after_start[:], position[:], starts_sb[:, b : b + 1], None, ALU.is_ge)
+            nc.vector.scalar_tensor_tensor(
+                out=mask[0][:, b * POSITIONS : (b + 1) * POSITIONS], in0=position[:],
+                scalar=ends_sb[:, b : b + 1], in1=after_start[:], op0=ALU.is_le, op1=ALU.mult,
+            )
 
         for cb in range(FEATURE_BLOCKS):
             rows = slice(cb * P, (cb + 1) * P)
@@ -89,22 +93,16 @@ def tile_nodeawaretokenembedder_kernel(tc, table, pos, node, starts, ends, offs,
                     ALU.add,
                 )
 
-            span = [psum.tile([P, BANK], F32, name=f"span{q}") for q in range(BANKS_PER_BLOCK)]
-            for k in range(NODE_BLOCKS):
-                for q in range(BANKS_PER_BLOCK):
-                    nc.tensor.matmul(
-                        span[q][:], node_sb[:, k, rows], mask[k][:, q * BANK : (q + 1) * BANK],
-                        start=(k == 0), stop=(k == NODE_BLOCKS - 1),
-                    )
-
-            span_sb = held.tile([P, TOKENS], F32, name=f"span_sb{cb}")
             for q in range(BANKS_PER_BLOCK):
                 cols = slice(q * BANK, (q + 1) * BANK)
-                if q == BANKS_PER_BLOCK - 1:
-                    nc.vector.tensor_tensor(embed[:, cols], embed[:, cols], span[q][:], ALU.add)
-                else:
-                    nc.scalar.copy(span_sb[:, cols], span[q][:])
-                    nc.gpsimd.tensor_tensor(embed[:, cols], embed[:, cols], span_sb[:, cols], ALU.add)
+                span = psum.tile([P, BANK], F32, name="span")
+                for k in range(NODE_BLOCKS):
+                    nc.tensor.matmul(
+                        span[:], node_sb[:, k, rows], mask[k][:, cols],
+                        start=(k == 0), stop=(k == NODE_BLOCKS - 1),
+                    )
+                nc.vector.tensor_tensor(embed[:, cols], embed[:, cols], span[:], ALU.add)
+
             for b in range(SEQS):
                 cols = slice(b * POSITIONS, (b + 1) * POSITIONS)
                 nc.sync.dma_start(out[rows, cols], embed[:, cols])

@@ -1,4 +1,5 @@
 import concourse.mybir as mybir
+from concourse.masks import make_identity
 
 F32 = mybir.dt.float32
 BF16 = mybir.dt.bfloat16
@@ -19,6 +20,7 @@ BANK = 512
 BANKS_PER_BLOCK = TOKENS // BANK
 PSUM_BANKS = 8
 OFFSET_COLS = POSITIONS // 16
+TENSOR_BANK = 0
 
 FLOPS = 2 * NODES * FEATURES * TOKENS
 
@@ -81,6 +83,9 @@ def tile_nodeawaretokenembedder_kernel(tc, table, pos, node, starts, ends, offs,
                 scalar=ends_sb[:, b : b + 1], in1=after_start[:], op0=ALU.is_le, op1=ALU.mult,
             )
 
+        identity = held.tile([P, P], F32, name="identity")
+        make_identity(nc, identity[:])
+
         for cb in range(FEATURE_BLOCKS):
             rows = slice(cb * P, (cb + 1) * P)
 
@@ -93,16 +98,21 @@ def tile_nodeawaretokenembedder_kernel(tc, table, pos, node, starts, ends, offs,
                     ALU.add,
                 )
 
+            spans = []
             for q in range(BANKS_PER_BLOCK):
-                cols = slice(q * BANK, (q + 1) * BANK)
                 span = psum.tile([P, BANK], F32, name="span")
                 for k in range(NODE_BLOCKS):
                     nc.tensor.matmul(
-                        span[:], node_sb[:, k, rows], mask[k][:, cols],
-                        start=(k == 0), stop=(k == NODE_BLOCKS - 1),
+                        span[:], node_sb[:, k, rows], mask[k][:, q * BANK : (q + 1) * BANK],
+                        start=(k == 0), stop=(k == NODE_BLOCKS - 1 and q != TENSOR_BANK),
                     )
-                nc.vector.tensor_tensor(embed[:, cols], embed[:, cols], span[:], ALU.add)
+                spans.append(span)
 
-            for b in range(SEQS):
-                cols = slice(b * POSITIONS, (b + 1) * POSITIONS)
+            for q in range(BANKS_PER_BLOCK):
+                cols = slice(q * BANK, (q + 1) * BANK)
+                if q == TENSOR_BANK:
+                    nc.tensor.matmul(spans[q][:], identity[:], embed[:, cols], start=False, stop=True)
+                    nc.scalar.copy(embed[:, cols], spans[q][:])
+                else:
+                    nc.vector.tensor_tensor(embed[:, cols], embed[:, cols], spans[q][:], ALU.add)
                 nc.sync.dma_start(out[rows, cols], embed[:, cols])

@@ -36,22 +36,26 @@ def tile_nodeawaretokenembedder_kernel(tc, table, pos, node, starts, ends, offs,
         nc.scalar.activation(warm[:], warm[:], ABS)
 
         offsets = held.tile([P, TOKENS // 16], U16, name="offsets")
-        nc.sync.dma_start(offsets[:], offs)
 
         starts_sb = held.tile([P, NODE_BLOCKS * SEQS], F32, name="starts_sb")
         ends_sb = held.tile([P, NODE_BLOCKS * SEQS], F32, name="ends_sb")
         node_sb = held.tile([P, NODE_BLOCKS, FEATURES], BF16, name="node_sb")
         nc.sync.dma_start(starts_sb[:], starts.rearrange("(p k) b -> p (k b)", k=NODE_BLOCKS))
         nc.sync.dma_start(ends_sb[:], ends.rearrange("(p k) b -> p (k b)", k=NODE_BLOCKS))
-        nc.sync.dma_start(node_sb[:], node.rearrange("(p k) c -> p k c", k=NODE_BLOCKS))
+        node_by_partition = node.rearrange("(p k) c -> p k c", k=NODE_BLOCKS)
         pos_sb = []
         table_sb = []
         for cb in range(FEATURE_BLOCKS):
             rows = slice(cb * P, (cb + 1) * P)
+            if cb == 0:
+                nc.sync.dma_start(node_sb[:, :, rows], node_by_partition[:, :, rows])
+                nc.sync.dma_start(offsets[:], offs)
             pos_sb.append(held.tile([P, POSITIONS], F32, name=f"pos{cb}"))
             nc.sync.dma_start(pos_sb[cb][:], pos[rows, :])
             table_sb.append(held.tile([P, VOCAB], F32, name=f"table{cb}"))
             nc.sync.dma_start(table_sb[cb][:], table[rows, :])
+            if cb == 0:
+                nc.sync.dma_start(node_sb[:, :, P:], node_by_partition[:, :, P:])
 
         position = held.tile([P, POSITIONS], F32, name="position")
         nc.gpsimd.iota(

@@ -18,11 +18,15 @@ FEATURE_BLOCKS = FEATURES // P
 NODE_BLOCKS = NODES // P
 BANK = 512
 BANKS_PER_BLOCK = TOKENS // BANK
+BANKS_PER_SEQ = POSITIONS // BANK
 PSUM_BANKS = 8
 OFFSET_COLS = POSITIONS // 16
-TENSOR_BANK = 0
 
 FLOPS = 2 * NODES * FEATURES * TOKENS
+
+
+def on_tensor(cb, q):
+    return q % BANKS_PER_SEQ == 0 and 0 < cb < FEATURE_BLOCKS - 1
 
 
 def tile_nodeawaretokenembedder_kernel(tc, table, pos, node, starts, ends, offs, out):
@@ -108,13 +112,13 @@ def tile_nodeawaretokenembedder_kernel(tc, table, pos, node, starts, ends, offs,
                 for k in range(NODE_BLOCKS):
                     nc.tensor.matmul(
                         span[:], node_sb[:, k, rows], mask[k][:, q * BANK : (q + 1) * BANK],
-                        start=(k == 0), stop=(k == NODE_BLOCKS - 1 and q != TENSOR_BANK),
+                        start=(k == 0), stop=(k == NODE_BLOCKS - 1 and not on_tensor(cb, q)),
                     )
                 spans.append(span)
 
             for q in range(BANKS_PER_BLOCK):
                 cols = slice(q * BANK, (q + 1) * BANK)
-                if q == TENSOR_BANK:
+                if on_tensor(cb, q):
                     nc.tensor.matmul(spans[q][:], identity[:], embed[:, cols], start=False, stop=True)
                     nc.scalar.copy(embed[:, cols], spans[q][:])
                 else:

@@ -26,7 +26,7 @@ FLOPS = 2 * NODES * FEATURES * TOKENS
 
 
 def on_tensor(cb, q):
-    return q % BANKS_PER_SEQ == 0 and 0 < cb < FEATURE_BLOCKS - 1
+    return q % BANKS_PER_SEQ == 0 and cb < FEATURE_BLOCKS - 1
 
 
 def tile_nodeawaretokenembedder_kernel(tc, table, pos, node, starts, ends, offs, out):

import concourse.mybir as mybir
from concourse.masks import make_identity

F32 = mybir.dt.float32
BF16 = mybir.dt.bfloat16
U16 = mybir.dt.uint16
ALU = mybir.AluOpType
ABS = mybir.ActivationFunctionType.Abs

P = 128
FEATURES = 512
VOCAB = 4096
SEQS = 2
POSITIONS = 1024
TOKENS = SEQS * POSITIONS
NODES = 512
FEATURE_BLOCKS = FEATURES // P
NODE_BLOCKS = NODES // P
BANK = 512
BANKS_PER_BLOCK = TOKENS // BANK
BANKS_PER_SEQ = POSITIONS // BANK
PSUM_BANKS = 8
OFFSET_COLS = POSITIONS // 16

FLOPS = 2 * NODES * FEATURES * TOKENS


def on_tensor(cb, q):
    return q % BANKS_PER_SEQ == 0 and cb < FEATURE_BLOCKS - 1


def tile_nodeawaretokenembedder_kernel(tc, table, pos, node, starts, ends, offs, out):
    nc = tc.nc
    with (
        tc.tile_pool(name="held", bufs=1) as held,
        tc.psum_pool(name="psum", bufs=PSUM_BANKS) as psum,
    ):
        warm = held.tile([P, 1], F32, name="warm")
        nc.vector.memset(warm[:], 0.0)
        nc.scalar.activation(warm[:], warm[:], ABS)

        offsets = held.tile([P, TOKENS // 16], U16, name="offsets")

        starts_sb = held.tile([P, NODE_BLOCKS * SEQS], F32, name="starts_sb")
        ends_sb = held.tile([P, NODE_BLOCKS * SEQS], F32, name="ends_sb")
        node_sb = held.tile([P, NODE_BLOCKS, FEATURES], BF16, name="node_sb")
        nc.sync.dma_start(starts_sb[:], starts.rearrange("(p k) b -> p (k b)", k=NODE_BLOCKS))
        nc.sync.dma_start(ends_sb[:], ends.rearrange("(p k) b -> p (k b)", k=NODE_BLOCKS))
        node_by_partition = node.rearrange("(p k) c -> p k c", k=NODE_BLOCKS)
        pos_sb = []
        table_sb = []
        for cb in range(FEATURE_BLOCKS):
            rows = slice(cb * P, (cb + 1) * P)
            if cb == 0:
                nc.sync.dma_start(node_sb[:, :, rows], node_by_partition[:, :, rows])
                nc.sync.dma_start(offsets[:], offs)
            pos_sb.append(held.tile([P, POSITIONS], F32, name=f"pos{cb}"))
            nc.sync.dma_start(pos_sb[cb][:], pos[rows, :])
            table_sb.append(held.tile([P, VOCAB], F32, name=f"table{cb}"))
            nc.sync.dma_start(table_sb[cb][:], table[rows, :])
            if cb == 0:
                nc.sync.dma_start(node_sb[:, :, P:], node_by_partition[:, :, P:])

        position = held.tile([P, POSITIONS], F32, name="position")
        nc.gpsimd.iota(
            position[:], pattern=[[1, POSITIONS]], base=0, channel_multiplier=0,
            allow_small_or_imprecise_dtypes=True,
        )
        mask = [held.tile([P, TOKENS], BF16, name=f"mask{k}") for k in range(NODE_BLOCKS)]

        neg_sum = held.tile([P, NODE_BLOCKS * SEQS], F32, name="neg_sum")
        nc.vector.scalar_tensor_tensor(
            out=neg_sum[:], in0=starts_sb[:], scalar=-1.0, in1=ends_sb[:], op0=ALU.mult, op1=ALU.subtract
        )
        length = held.tile([P, NODE_BLOCKS * SEQS], F32, name="length")
        nc.vector.tensor_tensor(length[:], ends_sb[:], starts_sb[:], ALU.subtract)
        for b in range(SEQS):
            for k in range(1, NODE_BLOCKS):
                col = k * SEQS + b
                distance = held.tile([P, POSITIONS], F32, name=f"distance{k}_{b}")
                nc.scalar.activation(distance[:], position[:], ABS, bias=neg_sum[:, col : col + 1], scale=2.0)
                nc.vector.tensor_scalar(
                    mask[k][:, b * POSITIONS : (b + 1) * POSITIONS], distance[:],
                    length[:, col : col + 1], None, ALU.is_le,
                )
        for b in range(SEQS):
            after_start = held.tile([P, POSITIONS], BF16, name=f"after_start{b}")
            nc.vector.tensor_scalar(after_start[:], position[:], starts_sb[:, b : b + 1], None, ALU.is_ge)
            nc.vector.scalar_tensor_tensor(
                out=mask[0][:, b * POSITIONS : (b + 1) * POSITIONS], in0=position[:],
                scalar=ends_sb[:, b : b + 1], in1=after_start[:], op0=ALU.is_le, op1=ALU.mult,
            )

        identity = held.tile([P, P], F32, name="identity")
        make_identity(nc, identity[:])

        for cb in range(FEATURE_BLOCKS):
            rows = slice(cb * P, (cb + 1) * P)

            embed = held.tile([P, TOKENS], F32, name=f"embed{cb}")
            for b in range(SEQS):
                nc.vector.tensor_tensor(
                    embed[:, b * POSITIONS : (b + 1) * POSITIONS],
                    table_sb[cb][:].indirect(offsets[:, b * OFFSET_COLS : (b + 1) * OFFSET_COLS]),
                    pos_sb[cb][:],
                    ALU.add,
                )

            spans = []
            for q in range(BANKS_PER_BLOCK):
                span = psum.tile([P, BANK], F32, name="span")
                for k in range(NODE_BLOCKS):
                    nc.tensor.matmul(
                        span[:], node_sb[:, k, rows], mask[k][:, q * BANK : (q + 1) * BANK],
                        start=(k == 0), stop=(k == NODE_BLOCKS - 1 and not on_tensor(cb, q)),
                    )
                spans.append(span)

            for q in range(BANKS_PER_BLOCK):
                cols = slice(q * BANK, (q + 1) * BANK)
                if on_tensor(cb, q):
                    nc.tensor.matmul(spans[q][:], identity[:], embed[:, cols], start=False, stop=True)
                    nc.scalar.copy(embed[:, cols], spans[q][:])
                else:
                    nc.vector.tensor_tensor(embed[:, cols], embed[:, cols], spans[q][:], ALU.add)
                nc.sync.dma_start(out[rows, cols], embed[:, cols])
